import numpy as np
import ml_dtypes


def mxq(x, axis, fmt="e4m3"):
    dtype, down = {"e4m3": (ml_dtypes.float8_e4m3fn, 7), "e5m2": (ml_dtypes.float8_e5m2, 14)}[fmt]
    v = np.moveaxis(np.asarray(x, np.float32).astype(ml_dtypes.bfloat16).astype(np.float64), axis, -1)
    blocks = v.reshape(v.shape[:-1] + (-1, 32))
    amax = np.abs(blocks).max(-1, keepdims=True)
    byte = np.maximum(np.where(amax > 0, np.frexp(amax)[1] - 1 + 127, 0) - down, 1)
    scale = np.exp2(byte - 127.0)
    codes = (blocks / scale).astype(np.float32).astype(dtype).astype(np.float64)
    return np.moveaxis((codes * scale).reshape(v.shape), -1, axis)


WIDE = False


def mx_kscale(k):
    if not WIDE:
        return np.ones(k)
    levels = np.array([10, -10, 5, -5, 0])
    a = np.random.permutation(np.resize(levels, k // 512 * 4)).reshape(k // 512, 4)
    idx = np.arange(k)
    return np.exp2(a[idx // 512, idx % 128 // 32])


BF16 = ml_dtypes.bfloat16


def bf(x):
    return np.asarray(x, np.float32).astype(BF16)


def f64(x):
    return np.asarray(x).astype(np.float64)


B, IN_DIM, LAT, OUT_DIM = 8192, 256, 256, 512
G = IN_DIM + LAT


def sigmoid(v):
    return 1.0 / (1.0 + np.exp(-v))


def setup_inputs():
    s = mx_kscale(G)
    return {
        "x_t": bf(np.random.standard_normal((B, IN_DIM)) * s[:IN_DIM]),
        "h_t": bf(np.random.standard_normal((B, LAT)) * 0.85 * s[IN_DIM:]),
        "Wy": bf(np.random.standard_normal((G, OUT_DIM)) * 0.8 / np.sqrt(G) / s[:, None]),
        "by": bf(np.random.standard_normal(OUT_DIM) * 0.2),
        "Wo": bf(np.random.standard_normal((G, OUT_DIM)) * 0.8 / np.sqrt(G) / s[:, None]),
        "bo": bf(np.random.standard_normal(OUT_DIM) * 0.2),
    }


def reference(x_t, h_t, Wy, by, Wo, bo):
    xq = mxq(np.concatenate([f64(x_t), f64(h_t)], axis=1), 1, "e4m3")
    y_hat = np.tanh((xq @ mxq(f64(Wy), 0, "e4m3")) + f64(by))
    o_t = sigmoid((xq @ mxq(f64(Wo), 0, "e4m3")) + f64(bo))
    return y_hat * o_t

@@ -1,0 +1,241 @@
+from contextlib import ExitStack
+
+import concourse.mybir as mybir
+from concourse.masks import make_identity
+
+FP8X4 = mybir.dt.float8_e4m3fn_x4
+BF16 = mybir.dt.bfloat16
+F32 = mybir.dt.float32
+U32 = mybir.dt.uint32
+U8 = mybir.dt.uint8
+ACT = mybir.ActivationFunctionType
+ALU = mybir.AluOpType
+
+P = 128
+ROWS = 8192
+HALF_K = 256
+N_OUT = 512
+TILES = ROWS // P
+GROUP = 4
+GROUPS = TILES // GROUP
+GCOLS = GROUP * N_OUT
+LOAD_CHUNKS = (1, 1, 2, 4, 4, 4)
+V_COPIES = ((5, 1), (9, 1), (13, 1))
+MX_RING = 4
+
+FLOPS = 2 * ROWS * (2 * HALF_K) * (2 * N_OUT)
+
+
+def tile_gatel0rdcell_pb_t_kernel(tc, x_t, h_t, Wy, by, Wo, bo, out):
+    nc = tc.nc
+    x_v = x_t.rearrange("(p j) k -> p (j k)", j=TILES)
+    h_v = h_t.rearrange("(p j) k -> p (j k)", j=TILES)
+    out_v = out.rearrange("(p j) c -> p (j c)", j=TILES)
+
+    with ExitStack() as ctx:
+        const = ctx.enter_context(tc.tile_pool(name="const", bufs=1))
+        stage = ctx.enter_context(tc.tile_pool(name="stage", bufs=4))
+        work = ctx.enter_context(tc.tile_pool(name="work", bufs=5))
+        psum_t = ctx.enter_context(tc.psum_pool(name="psum_t", bufs=4))
+        psum_m = ctx.enter_context(tc.psum_pool(name="psum_m", bufs=MX_RING))
+        ctx.enter_context(tc.manual_schedule())
+
+        brow = const.tile([P, 2 * N_OUT], BF16, name="brow")
+        ones = const.tile([P, P], BF16, name="ones")
+        warm = const.tile([P, 8], F32, name="warm")
+        ident = const.tile([P, P], F32, name="ident")
+        nc.vector.memset(brow[:], 0.0)
+        nc.vector.memset(ones[:], 1.0)
+        nc.vector.memset(warm[:], 0.0)
+        make_identity(nc, ident[:])
+        nc.scalar.dma_start(out=brow[0:1, 0:N_OUT], in_=by.rearrange("(o n) -> o n", o=1))
+        nc.scalar.dma_start(out=brow[0:1, N_OUT : 2 * N_OUT], in_=bo.rearrange("(o n) -> o n", o=1))
+        nc.scalar.activation(out=warm[:, 4:8], in_=warm[:, 0:4], func=ACT.Sigmoid)
+
+        x_of = {}
+        w_raw = {}
+
+        def load_rows(first_group, n_groups):
+            width = n_groups * GROUP * HALF_K
+            lo = first_group * GROUP * HALF_K
+            xs = const.tile([P, width], BF16, name="x%d" % first_group)
+            hs = const.tile([P, width], BF16, name="h%d" % first_group)
+            nc.sync.dma_start(out=xs[:], in_=x_v[:, lo : lo + width])
+            nc.sync.dma_start(out=hs[:], in_=h_v[:, lo : lo + width])
+            for i in range(n_groups):
+                x_of[first_group + i] = (xs, hs, i)
+
+        def load_w(key, w):
+            raw = const.tile([P, 4 * N_OUT], BF16, name="raw_" + key)
+            nc.sync.dma_start(
+                out=raw[:].rearrange("p (u f) -> p u f", u=2),
+                in_=w.rearrange("(u p e) n -> p u (e n)", u=2, e=2),
+            )
+            w_raw[key] = raw
+
+        load_rows(0, LOAD_CHUNKS[0])
+        load_w("y", Wy)
+        load_w("o", Wo)
+        first = LOAD_CHUNKS[0]
+        for n_groups in LOAD_CHUNKS[1:]:
+            load_rows(first, n_groups)
+            first += n_groups
+
+        banks = {}
+        grouped = {}
+        codes = {}
+        acc = {}
+        pre = {}
+        w_q = {}
+        bias = {}
+
+        def transposes(g):
+            xs, hs, i = x_of[g]
+            for b in range(2):
+                pt = psum_t.tile([P, 2, 2 * P], F32, name="pt", tag="pt")
+                for u, src in enumerate((xs, hs)):
+                    words = src[:].bitcast(F32)
+                    for jl in range(2):
+                        j = i * GROUP + 2 * b + jl
+                        nc.tensor.transpose(pt[:, u, jl * P : (jl + 1) * P], words[:, j * P : (j + 1) * P], ident[:])
+                banks[(g, b)] = pt
+
+        def copies(g):
+            gr = stage.tile([P, 4 * GROUP * P], BF16, name="gr", tag="gr", align_bytes=64)
+            words = gr[:].bitcast(F32).rearrange("p (n u) -> p n u", u=2)
+            for b in range(2):
+                src = banks[(g, b)][:].rearrange("p u n -> p n u")
+                dst = words[:, 2 * P * b : 2 * P * (b + 1), :]
+                if (g, b) in V_COPIES:
+                    nc.vector.tensor_copy(out=dst, in_=src)
+                else:
+                    nc.scalar.copy(out=dst, in_=src)
+            grouped[g] = gr
+
+        def quantise(g):
+            cw = stage.tile([P, GROUP * P], U32, name="cw", tag="cw", align_bytes=64)
+            cs = stage.tile([P, GROUP * P], U8, name="cs", tag="cs", align_bytes=64)
+            nc.vector.quantize_mx(out=cw[:].bitcast(FP8X4), scales=cs[:], in_=grouped[g][:])
+            codes[g] = (cw, cs)
+
+        def regroup_w(key, engine_copy):
+            gw = const.tile([P, 4 * N_OUT], BF16, name="gw_" + key, align_bytes=64)
+            engine_copy(
+                out=gw[:].rearrange("p (c i t) -> p c t i", i=4, t=4),
+                in_=w_raw[key][:].rearrange("p (t c i) -> p c t i", t=4, i=4),
+            )
+            grouped["w" + key] = gw
+
+        def quantise_w(key):
+            cw = const.tile([P, N_OUT], U32, name="wcw_" + key, align_bytes=64)
+            cs = const.tile([P, N_OUT], U8, name="wcs_" + key, align_bytes=64)
+            nc.vector.quantize_mx(out=cw[:].bitcast(FP8X4), scales=cs[:], in_=grouped["w" + key][:])
+            w_q[key] = (cw, cs)
+
+        def spread_bias(key, lo):
+            pb = psum_m.tile([P, N_OUT], F32, name="acc", tag="acc")
+            nc.tensor.matmul(pb[:], lhsT=ones[:], rhs=brow[:, lo : lo + N_OUT], start=True, stop=True)
+            bt = const.tile([P, N_OUT], F32, name="bias_" + key)
+            nc.scalar.copy(out=bt[:], in_=pb[:])
+            bias[key] = bt
+
+        def one_pass(g, j, key):
+            cw, cs = codes[g]
+            wc, ws = w_q[key]
+            a = psum_m.tile([P, N_OUT], F32, name="acc", tag="acc")
+            nc.tensor.matmul_mx(
+                out=a[:],
+                lhsT=cw[:, j * P : (j + 1) * P].bitcast(FP8X4),
+                lhsT_scale=cs[:, j * P : (j + 1) * P],
+                rhs=wc[:].bitcast(FP8X4),
+                rhs_scale=ws[:],
+                start=True,
+                stop=True,
+            )
+            acc[(g, j, key)] = a
+
+        def fill():
+            while count["issued"] < count["ready"] and count["issued"] - count["drained"] < MX_RING:
+                g, j, key = all_passes[count["issued"]]
+                one_pass(g, j, key)
+                count["issued"] += 1
+
+        def add_bias(g, j, key):
+            if g not in pre:
+                ty = work.tile([P, GCOLS], F32, name="ty", tag="ty")
+                to = work.tile([P, GCOLS], F32, name="to", tag="to")
+                pre[g] = {"y": ty, "o": to}
+            nc.vector.tensor_tensor(
+                out=pre[g][key][:, j * N_OUT : (j + 1) * N_OUT], in0=acc[(g, j, key)][:], in1=bias[key][:], op=ALU.add
+            )
+            count["drained"] += 1
+            fill()
+
+        def activate(g, lo, n):
+            sl = slice(lo * N_OUT, (lo + n) * N_OUT)
+            nc.scalar.activation(out=pre[g]["y"][:, sl], in_=pre[g]["y"][:, sl], func=ACT.Tanh)
+            nc.scalar.activation(out=pre[g]["o"][:, sl], in_=pre[g]["o"][:, sl], func=ACT.Sigmoid)
+
+        def multiply(g, lo, n, engine):
+            sl = slice(lo * N_OUT, (lo + n) * N_OUT)
+            engine.tensor_tensor(out=pre[g]["y"][:, sl], in0=pre[g]["y"][:, sl], in1=pre[g]["o"][:, sl], op=ALU.mult)
+
+        def store(g, lo, n):
+            sl = slice(lo * N_OUT, (lo + n) * N_OUT)
+            d0 = (g * GROUP + lo) * N_OUT
+            nc.sync.dma_start(out=out_v[:, d0 : d0 + n * N_OUT], in_=pre[g]["y"][:, sl])
+
+        by_tile = [(j, key) for j in range(GROUP) for key in ("y", "o")]
+        y_first = [(j, "y") for j in range(GROUP)] + [(j, "o") for j in range(GROUP)]
+        order_of = [y_first] + [by_tile] * (GROUPS - 1)
+        all_passes = [(g, j, key) for g in range(GROUPS) for j, key in order_of[g]]
+        count = {"issued": 0, "ready": 0, "drained": 0}
+        last = GROUPS - 1
+
+        spread_bias("y", 0)
+        spread_bias("o", N_OUT)
+        transposes(0)
+        copies(0)
+        regroup_w("y", nc.vector.tensor_copy)
+        regroup_w("o", nc.scalar.copy)
+        quantise(0)
+        quantise_w("y")
+        transposes(1)
+        copies(1)
+        count["ready"] = GROUP
+        fill()
+
+        for g in range(GROUPS):
+            for k, (j, key) in enumerate(order_of[g]):
+                add_bias(g, j, key)
+                if g == 0 and k == 0:
+                    quantise_w("o")
+                    count["ready"] = 2 * GROUP
+                    fill()
+                if k == GROUP - 1 and g < last:
+                    quantise(g + 1)
+                    if g == 0:
+                        transposes(2)
+                    if g + 3 < GROUPS:
+                        transposes(g + 3)
+                    count["ready"] += 2 * GROUP
+                    fill()
+            if g == 0:
+                copies(2)
+            if g < last:
+                activate(g, 0, 2)
+                if g + 3 < GROUPS:
+                    copies(g + 3)
+                activate(g, 2, 2)
+                if g < last - 1:
+                    multiply(g, 0, GROUP, nc.gpsimd)
+                    store(g, 0, GROUP)
+                else:
+                    for lo in (0, 2):
+                        multiply(g, lo, 2, nc.gpsimd)
+                        store(g, lo, 2)
+            else:
+                for j in range(GROUP):
+                    activate(g, j, 1)
+                    multiply(g, j, 1, nc.vector)
+                    store(g, j, 1)

@@ -18,10 +18,10 @@ N_OUT = 512
 TILES = ROWS // P
 GROUP = 4
 GROUPS = TILES // GROUP
-GCOLS = GROUP * N_OUT
-LOAD_CHUNKS = (1, 1, 2, 4, 4, 4)
-V_COPIES = ((5, 1), (9, 1), (13, 1))
-MX_RING = 4
+GROWS = GROUP * P
+BLOCKS = N_OUT // P
+LOAD_CHUNKS = (1, 1, 1, 1, 2, 2, 4, 4)
+FUNCS = (("y", ACT.Tanh), ("o", ACT.Sigmoid))
 
 FLOPS = 2 * ROWS * (2 * HALF_K) * (2 * N_OUT)
 
@@ -34,22 +34,22 @@ def tile_gatel0rdcell_pb_t_kernel(tc, x_t, h_t, Wy, by, Wo, bo, out):
 
     with ExitStack() as ctx:
         const = ctx.enter_context(tc.tile_pool(name="const", bufs=1))
-        stage = ctx.enter_context(tc.tile_pool(name="stage", bufs=4))
-        work = ctx.enter_context(tc.tile_pool(name="work", bufs=5))
+        stage = ctx.enter_context(tc.tile_pool(name="stage", bufs=3))
+        work = ctx.enter_context(tc.tile_pool(name="work", bufs=4))
         psum_t = ctx.enter_context(tc.psum_pool(name="psum_t", bufs=4))
-        psum_m = ctx.enter_context(tc.psum_pool(name="psum_m", bufs=MX_RING))
+        psum_m = ctx.enter_context(tc.psum_pool(name="psum_m", bufs=4))
         ctx.enter_context(tc.manual_schedule())
 
-        brow = const.tile([P, 2 * N_OUT], BF16, name="brow")
-        ones = const.tile([P, P], BF16, name="ones")
+        brow = const.tile([2 * BLOCKS, P], BF16, name="brow")
+        brow32 = const.tile([P, P], F32, name="brow32")
+        bias = const.tile([P, 2 * BLOCKS], F32, name="bias")
         warm = const.tile([P, 8], F32, name="warm")
         ident = const.tile([P, P], F32, name="ident")
-        nc.vector.memset(brow[:], 0.0)
-        nc.vector.memset(ones[:], 1.0)
+        nc.scalar.dma_start(out=brow[0:BLOCKS, :], in_=by.rearrange("(r m) -> r m", r=BLOCKS))
+        nc.scalar.dma_start(out=brow[BLOCKS : 2 * BLOCKS, :], in_=bo.rearrange("(r m) -> r m", r=BLOCKS))
         nc.vector.memset(warm[:], 0.0)
+        nc.vector.memset(brow32[:], 0.0)
         make_identity(nc, ident[:])
-        nc.scalar.dma_start(out=brow[0:1, 0:N_OUT], in_=by.rearrange("(o n) -> o n", o=1))
-        nc.scalar.dma_start(out=brow[0:1, N_OUT : 2 * N_OUT], in_=bo.rearrange("(o n) -> o n", o=1))
         nc.scalar.activation(out=warm[:, 4:8], in_=warm[:, 0:4], func=ACT.Sigmoid)
 
         x_of = {}
@@ -85,157 +85,183 @@ def tile_gatel0rdcell_pb_t_kernel(tc, x_t, h_t, Wy, by, Wo, bo, out):
         grouped = {}
         codes = {}
         acc = {}
-        pre = {}
+        gate = {}
+        turned = {}
+        result = {}
         w_q = {}
-        bias = {}
 
-        def transposes(g):
+        def ok(g):
+            return 0 <= g < GROUPS
+
+        def transposes_in(g, b):
             xs, hs, i = x_of[g]
-            for b in range(2):
-                pt = psum_t.tile([P, 2, 2 * P], F32, name="pt", tag="pt")
-                for u, src in enumerate((xs, hs)):
-                    words = src[:].bitcast(F32)
-                    for jl in range(2):
-                        j = i * GROUP + 2 * b + jl
-                        nc.tensor.transpose(pt[:, u, jl * P : (jl + 1) * P], words[:, j * P : (j + 1) * P], ident[:])
-                banks[(g, b)] = pt
+            pt = psum_t.tile([P, 2, 2 * P], F32, name="pt", tag="pt")
+            for u, src in enumerate((xs, hs)):
+                words = src[:].bitcast(F32)
+                for jl in range(2):
+                    j = i * GROUP + 2 * b + jl
+                    nc.tensor.transpose(pt[:, u, jl * P : (jl + 1) * P], words[:, j * P : (j + 1) * P], ident[:])
+            banks[(g, b)] = pt
 
-        def copies(g):
-            gr = stage.tile([P, 4 * GROUP * P], BF16, name="gr", tag="gr", align_bytes=64)
-            words = gr[:].bitcast(F32).rearrange("p (n u) -> p n u", u=2)
-            for b in range(2):
-                src = banks[(g, b)][:].rearrange("p u n -> p n u")
-                dst = words[:, 2 * P * b : 2 * P * (b + 1), :]
-                if (g, b) in V_COPIES:
-                    nc.vector.tensor_copy(out=dst, in_=src)
-                else:
-                    nc.scalar.copy(out=dst, in_=src)
-            grouped[g] = gr
+        def copy_in(g, b, engine_copy):
+            if g not in grouped:
+                gr = stage.tile([P, 4 * GROWS], BF16, name="gr", tag="gr", align_bytes=64)
+                grouped[g] = gr
+            words = grouped[g][:].bitcast(F32).rearrange("p (n u) -> p n u", u=2)
+            engine_copy(out=words[:, 2 * P * b : 2 * P * (b + 1), :], in_=banks[(g, b)][:].rearrange("p u n -> p n u"))
 
         def quantise(g):
-            cw = stage.tile([P, GROUP * P], U32, name="cw", tag="cw", align_bytes=64)
-            cs = stage.tile([P, GROUP * P], U8, name="cs", tag="cs", align_bytes=64)
+            cw = stage.tile([P, GROWS], U32, name="cw", tag="cw", align_bytes=64)
+            cs = stage.tile([P, GROWS], U8, name="cs", tag="cs", align_bytes=64)
             nc.vector.quantize_mx(out=cw[:].bitcast(FP8X4), scales=cs[:], in_=grouped[g][:])
             codes[g] = (cw, cs)
 
-        def regroup_w(key, engine_copy):
-            gw = const.tile([P, 4 * N_OUT], BF16, name="gw_" + key, align_bytes=64)
+        def regroup_w(key, h, engine_copy):
+            gw = const.tile([P, 2 * N_OUT], BF16, name="gw_%s%d" % (key, h), align_bytes=64)
+            half = w_raw[key][:].rearrange("p (t n) -> p t n", t=4)[:, :, h * 2 * P : (h + 1) * 2 * P]
             engine_copy(
                 out=gw[:].rearrange("p (c i t) -> p c t i", i=4, t=4),
-                in_=w_raw[key][:].rearrange("p (t c i) -> p c t i", t=4, i=4),
+                in_=half.rearrange("p t (c i) -> p c t i", i=4),
             )
-            grouped["w" + key] = gw
+            grouped[(key, h)] = gw
 
-        def quantise_w(key):
-            cw = const.tile([P, N_OUT], U32, name="wcw_" + key, align_bytes=64)
-            cs = const.tile([P, N_OUT], U8, name="wcs_" + key, align_bytes=64)
-            nc.vector.quantize_mx(out=cw[:].bitcast(FP8X4), scales=cs[:], in_=grouped["w" + key][:])
-            w_q[key] = (cw, cs)
+        def quantise_w(key, h):
+            cw = const.tile([P, 2 * P], U32, name="wcw_%s%d" % (key, h), align_bytes=64)
+            cs = const.tile([P, 2 * P], U8, name="wcs_%s%d" % (key, h), align_bytes=64)
+            nc.vector.quantize_mx(out=cw[:].bitcast(FP8X4), scales=cs[:], in_=grouped[(key, h)][:])
+            w_q[(key, h)] = (cw, cs)
 
-        def spread_bias(key, lo):
-            pb = psum_m.tile([P, N_OUT], F32, name="acc", tag="acc")
-            nc.tensor.matmul(pb[:], lhsT=ones[:], rhs=brow[:, lo : lo + N_OUT], start=True, stop=True)
-            bt = const.tile([P, N_OUT], F32, name="bias_" + key)
-            nc.scalar.copy(out=bt[:], in_=pb[:])
-            bias[key] = bt
-
-        def one_pass(g, j, key):
-            cw, cs = codes[g]
-            wc, ws = w_q[key]
-            a = psum_m.tile([P, N_OUT], F32, name="acc", tag="acc")
-            nc.tensor.matmul_mx(
-                out=a[:],
-                lhsT=cw[:, j * P : (j + 1) * P].bitcast(FP8X4),
-                lhsT_scale=cs[:, j * P : (j + 1) * P],
-                rhs=wc[:].bitcast(FP8X4),
-                rhs_scale=ws[:],
-                start=True,
-                stop=True,
-            )
-            acc[(g, j, key)] = a
-
-        def fill():
-            while count["issued"] < count["ready"] and count["issued"] - count["drained"] < MX_RING:
-                g, j, key = all_passes[count["issued"]]
-                one_pass(g, j, key)
-                count["issued"] += 1
-
-        def add_bias(g, j, key):
-            if g not in pre:
-                ty = work.tile([P, GCOLS], F32, name="ty", tag="ty")
-                to = work.tile([P, GCOLS], F32, name="to", tag="to")
-                pre[g] = {"y": ty, "o": to}
-            nc.vector.tensor_tensor(
-                out=pre[g][key][:, j * N_OUT : (j + 1) * N_OUT], in0=acc[(g, j, key)][:], in1=bias[key][:], op=ALU.add
-            )
-            count["drained"] += 1
-            fill()
-
-        def activate(g, lo, n):
-            sl = slice(lo * N_OUT, (lo + n) * N_OUT)
-            nc.scalar.activation(out=pre[g]["y"][:, sl], in_=pre[g]["y"][:, sl], func=ACT.Tanh)
-            nc.scalar.activation(out=pre[g]["o"][:, sl], in_=pre[g]["o"][:, sl], func=ACT.Sigmoid)
-
-        def multiply(g, lo, n, engine):
-            sl = slice(lo * N_OUT, (lo + n) * N_OUT)
-            engine.tensor_tensor(out=pre[g]["y"][:, sl], in0=pre[g]["y"][:, sl], in1=pre[g]["o"][:, sl], op=ALU.mult)
-
-        def store(g, lo, n):
-            sl = slice(lo * N_OUT, (lo + n) * N_OUT)
-            d0 = (g * GROUP + lo) * N_OUT
-            nc.sync.dma_start(out=out_v[:, d0 : d0 + n * N_OUT], in_=pre[g]["y"][:, sl])
-
-        by_tile = [(j, key) for j in range(GROUP) for key in ("y", "o")]
-        y_first = [(j, "y") for j in range(GROUP)] + [(j, "o") for j in range(GROUP)]
-        order_of = [y_first] + [by_tile] * (GROUPS - 1)
-        all_passes = [(g, j, key) for g in range(GROUPS) for j, key in order_of[g]]
-        count = {"issued": 0, "ready": 0, "drained": 0}
-        last = GROUPS - 1
-
-        spread_bias("y", 0)
-        spread_bias("o", N_OUT)
-        transposes(0)
-        copies(0)
-        regroup_w("y", nc.vector.tensor_copy)
-        regroup_w("o", nc.scalar.copy)
-        quantise(0)
-        quantise_w("y")
-        transposes(1)
-        copies(1)
-        count["ready"] = GROUP
-        fill()
-
-        for g in range(GROUPS):
-            for k, (j, key) in enumerate(order_of[g]):
-                add_bias(g, j, key)
-                if g == 0 and k == 0:
-                    quantise_w("o")
-                    count["ready"] = 2 * GROUP
-                    fill()
-                if k == GROUP - 1 and g < last:
-                    quantise(g + 1)
-                    if g == 0:
-                        transposes(2)
-                    if g + 3 < GROUPS:
-                        transposes(g + 3)
-                    count["ready"] += 2 * GROUP
-                    fill()
+        def order_of(g, h):
+            blocks = (2 * h, 2 * h + 1)
             if g == 0:
-                copies(2)
-            if g < last:
-                activate(g, 0, 2)
-                if g + 3 < GROUPS:
-                    copies(g + 3)
-                activate(g, 2, 2)
-                if g < last - 1:
-                    multiply(g, 0, GROUP, nc.gpsimd)
-                    store(g, 0, GROUP)
+                return [(c, f) for f in range(2) for c in blocks]
+            return [(c, f) for c in blocks for f in range(2)]
+
+        def passes(g, h):
+            cw, cs = codes[g]
+            for c, f in order_of(g, h):
+                wc, ws = w_q[(FUNCS[f][0], h)]
+                lo = (c - 2 * h) * P
+                a = psum_m.tile([P, GROWS], F32, name="acc", tag="acc")
+                nc.tensor.matmul_mx(
+                    out=a[:],
+                    lhsT=wc[:, lo : lo + P].bitcast(FP8X4),
+                    lhsT_scale=ws[:, lo : lo + P],
+                    rhs=cw[:].bitcast(FP8X4),
+                    rhs_scale=cs[:],
+                    start=True,
+                    stop=True,
+                )
+                acc[(g, c, f)] = a
+
+        def activate(g, h):
+            if g not in gate:
+                ty = work.tile([P, BLOCKS * GROWS], F32, name="ty", tag="ty")
+                to = work.tile([P, BLOCKS * GROWS], F32, name="to", tag="to")
+                gate[g] = (ty, to)
+            for c, f in order_of(g, h):
+                nc.scalar.activation(
+                    out=gate[g][f][:, c * GROWS : (c + 1) * GROWS],
+                    in_=acc[(g, c, f)][:],
+                    func=FUNCS[f][1],
+                    bias=bias[:, f * BLOCKS + c : f * BLOCKS + c + 1],
+                )
+
+        def multiply(g, c, n, engine):
+            sl = slice(c * GROWS, (c + n) * GROWS)
+            engine.tensor_tensor(out=gate[g][0][:, sl], in0=gate[g][0][:, sl], in1=gate[g][1][:, sl], op=ALU.mult)
+
+        def transposes_out(g, jl):
+            po = psum_t.tile([P, N_OUT], F32, name="po", tag="pt")
+            for c in range(BLOCKS):
+                lo = c * GROWS + jl * P
+                nc.tensor.transpose(po[:, c * P : (c + 1) * P], gate[g][0][:, lo : lo + P], ident[:])
+            turned[(g, jl)] = po
+
+        def copy_out(g, jl, engine_copy):
+            if g not in result:
+                res = work.tile([P, GROUP * N_OUT], F32, name="res", tag="res")
+                result[g] = res
+            engine_copy(out=result[g][:, jl * N_OUT : (jl + 1) * N_OUT], in_=turned[(g, jl)][:])
+
+        def store(g, jl, n):
+            d0 = (g * GROUP + jl) * N_OUT
+            nc.sync.dma_start(out=out_v[:, d0 : d0 + n * N_OUT], in_=result[g][:, jl * N_OUT : (jl + n) * N_OUT])
+
+        vcopy = nc.vector.tensor_copy
+        scopy = nc.scalar.copy
+
+        nc.vector.tensor_copy(out=brow32[0 : 2 * BLOCKS, :], in_=brow[:])
+        pb = psum_m.tile([P, GROWS], F32, name="acc", tag="acc")
+        nc.tensor.transpose(pb[:, 0:P], brow32[:], ident[:])
+        nc.vector.tensor_copy(out=bias[:], in_=pb[:, 0 : 2 * BLOCKS])
+        transposes_in(0, 0)
+        transposes_in(0, 1)
+        copy_in(0, 0, scopy)
+        copy_in(0, 1, scopy)
+        regroup_w("y", 0, vcopy)
+        quantise_w("y", 0)
+        quantise(0)
+        regroup_w("o", 0, scopy)
+        regroup_w("y", 1, vcopy)
+        quantise_w("o", 0)
+        passes(0, 0)
+        quantise_w("y", 1)
+        regroup_w("o", 1, vcopy)
+        quantise_w("o", 1)
+        transposes_in(1, 0)
+        transposes_in(1, 1)
+        copy_in(1, 0, vcopy)
+        copy_in(1, 1, vcopy)
+        quantise(1)
+
+        def tail(t):
+            return t + 2 >= GROUPS
+
+        for t in range(GROUPS + 1):
+            if ok(t):
+                activate(t, 0)
+                multiply(t, 0, 2, nc.gpsimd)
+            if ok(t + 2) and t > 0:
+                transposes_in(t + 2, 0)
+            if ok(t - 2) and not tail(t - 1):
+                transposes_out(t - 2, 2)
+                transposes_out(t - 2, 3)
+            if ok(t):
+                passes(t, 1)
+            if ok(t + 2) and t > 0:
+                copy_in(t + 2, 0, vcopy)
+            if ok(t - 2) and not tail(t - 1):
+                copy_out(t - 2, 2, vcopy)
+                copy_out(t - 2, 3, vcopy)
+                store(t - 2, 0, GROUP)
+            if ok(t):
+                activate(t, 1)
+                multiply(t, 2, 1, nc.gpsimd)
+            if ok(t + 2):
+                if t == 0:
+                    transposes_in(t + 2, 0)
+                transposes_in(t + 2, 1)
+            if ok(t - 1):
+                for jl in range(GROUP if tail(t) else 2):
+                    transposes_out(t - 1, jl)
+            if ok(t + 1):
+                passes(t + 1, 0)
+            if ok(t + 2):
+                if t == 0:
+                    copy_in(t + 2, 0, vcopy)
+                copy_in(t + 2, 1, vcopy)
+            if ok(t - 1):
+                if t == GROUPS:
+                    for jl in range(GROUP):
+                        copy_out(t - 1, jl, scopy if jl % 2 else vcopy)
+                        store(t - 1, jl, 1)
                 else:
-                    for lo in (0, 2):
-                        multiply(g, lo, 2, nc.gpsimd)
-                        store(g, lo, 2)
-            else:
-                for j in range(GROUP):
-                    activate(g, j, 1)
-                    multiply(g, j, 1, nc.vector)
-                    store(g, j, 1)
+                    for jl in range(GROUP if tail(t) else 2):
+                        copy_out(t - 1, jl, vcopy)
+                    if tail(t):
+                        store(t - 1, 0, GROUP)
+            if ok(t + 2):
+                quantise(t + 2)
+            if ok(t):
+                multiply(t, 3, 1, nc.gpsimd if t == 0 else nc.vector)

@@ -167,8 +167,8 @@ def tile_gatel0rdcell_pb_t_kernel(tc, x_t, h_t, Wy, by, Wo, bo, out):
                     bias=bias[:, f * BLOCKS + c : f * BLOCKS + c + 1],
                 )
 
-        def multiply(g, c, n, engine):
-            sl = slice(c * GROWS, (c + n) * GROWS)
+        def multiply(g, lo, n, engine):
+            sl = slice(lo, lo + n)
             engine.tensor_tensor(out=gate[g][0][:, sl], in0=gate[g][0][:, sl], in1=gate[g][1][:, sl], op=ALU.mult)
 
         def transposes_out(g, jl):
@@ -221,7 +221,7 @@ def tile_gatel0rdcell_pb_t_kernel(tc, x_t, h_t, Wy, by, Wo, bo, out):
         for t in range(GROUPS + 1):
             if ok(t):
                 activate(t, 0)
-                multiply(t, 0, 2, nc.gpsimd)
+                multiply(t, 0, 2 * GROWS, nc.gpsimd)
             if ok(t + 2) and t > 0:
                 transposes_in(t + 2, 0)
             if ok(t - 2) and not tail(t - 1):
@@ -237,7 +237,7 @@ def tile_gatel0rdcell_pb_t_kernel(tc, x_t, h_t, Wy, by, Wo, bo, out):
                 store(t - 2, 0, GROUP)
             if ok(t):
                 activate(t, 1)
-                multiply(t, 2, 1, nc.gpsimd)
+                multiply(t, 2 * GROWS, GROWS, nc.gpsimd)
             if ok(t + 2):
                 if t == 0:
                     transposes_in(t + 2, 0)
@@ -264,4 +264,5 @@ def tile_gatel0rdcell_pb_t_kernel(tc, x_t, h_t, Wy, by, Wo, bo, out):
             if ok(t + 2):
                 quantise(t + 2)
             if ok(t):
-                multiply(t, 3, 1, nc.gpsimd if t == 0 else nc.vector)
+                multiply(t, 3 * GROWS, GROWS // 2, nc.gpsimd)
+                multiply(t, 3 * GROWS + GROWS // 2, GROWS // 2, nc.gpsimd if t == 0 else nc.vector)

@@ -38,7 +38,6 @@ def tile_gatel0rdcell_pb_t_kernel(tc, x_t, h_t, Wy, by, Wo, bo, out):
         work = ctx.enter_context(tc.tile_pool(name="work", bufs=4))
         psum_t = ctx.enter_context(tc.psum_pool(name="psum_t", bufs=4))
         psum_m = ctx.enter_context(tc.psum_pool(name="psum_m", bufs=4))
-        ctx.enter_context(tc.manual_schedule())
 
         brow = const.tile([2 * BLOCKS, P], BF16, name="brow")
         brow32 = const.tile([P, P], F32, name="brow32")
@@ -167,8 +166,8 @@ def tile_gatel0rdcell_pb_t_kernel(tc, x_t, h_t, Wy, by, Wo, bo, out):
                     bias=bias[:, f * BLOCKS + c : f * BLOCKS + c + 1],
                 )
 
-        def multiply(g, lo, n, engine):
-            sl = slice(lo, lo + n)
+        def multiply(g, c, n, engine):
+            sl = slice(c * GROWS, (c + n) * GROWS)
             engine.tensor_tensor(out=gate[g][0][:, sl], in0=gate[g][0][:, sl], in1=gate[g][1][:, sl], op=ALU.mult)
 
         def transposes_out(g, jl):
@@ -221,7 +220,7 @@ def tile_gatel0rdcell_pb_t_kernel(tc, x_t, h_t, Wy, by, Wo, bo, out):
         for t in range(GROUPS + 1):
             if ok(t):
                 activate(t, 0)
-                multiply(t, 0, 2 * GROWS, nc.gpsimd)
+                multiply(t, 0, 2, nc.gpsimd)
             if ok(t + 2) and t > 0:
                 transposes_in(t + 2, 0)
             if ok(t - 2) and not tail(t - 1):
@@ -237,7 +236,7 @@ def tile_gatel0rdcell_pb_t_kernel(tc, x_t, h_t, Wy, by, Wo, bo, out):
                 store(t - 2, 0, GROUP)
             if ok(t):
                 activate(t, 1)
-                multiply(t, 2 * GROWS, GROWS, nc.gpsimd)
+                multiply(t, 2, 1, nc.gpsimd)
             if ok(t + 2):
                 if t == 0:
                     transposes_in(t + 2, 0)
@@ -264,5 +263,4 @@ def tile_gatel0rdcell_pb_t_kernel(tc, x_t, h_t, Wy, by, Wo, bo, out):
             if ok(t + 2):
                 quantise(t + 2)
             if ok(t):
-                multiply(t, 3 * GROWS, GROWS // 2, nc.gpsimd)
-                multiply(t, 3 * GROWS + GROWS // 2, GROWS // 2, nc.gpsimd if t == 0 else nc.vector)
+                multiply(t, 3, 1, nc.gpsimd if t == 0 else nc.vector)

@@ -38,6 +38,7 @@ def tile_gatel0rdcell_pb_t_kernel(tc, x_t, h_t, Wy, by, Wo, bo, out):
         work = ctx.enter_context(tc.tile_pool(name="work", bufs=4))
         psum_t = ctx.enter_context(tc.psum_pool(name="psum_t", bufs=4))
         psum_m = ctx.enter_context(tc.psum_pool(name="psum_m", bufs=4))
+        ctx.enter_context(tc.manual_schedule())
 
         brow = const.tile([2 * BLOCKS, P], BF16, name="brow")
         brow32 = const.tile([P, P], F32, name="brow32")
@@ -136,9 +137,9 @@ def tile_gatel0rdcell_pb_t_kernel(tc, x_t, h_t, Wy, by, Wo, bo, out):
                 return [(c, f) for f in range(2) for c in blocks]
             return [(c, f) for c in blocks for f in range(2)]
 
-        def passes(g, h):
+        def passes(g, h, first=0, n=4):
             cw, cs = codes[g]
-            for c, f in order_of(g, h):
+            for c, f in order_of(g, h)[first : first + n]:
                 wc, ws = w_q[(FUNCS[f][0], h)]
                 lo = (c - 2 * h) * P
                 a = psum_m.tile([P, GROWS], F32, name="acc", tag="acc")
@@ -201,15 +202,16 @@ def tile_gatel0rdcell_pb_t_kernel(tc, x_t, h_t, Wy, by, Wo, bo, out):
         regroup_w("y", 0, vcopy)
         quantise_w("y", 0)
         quantise(0)
+        passes(0, 0, 0, 2)
+        transposes_in(1, 0)
+        transposes_in(1, 1)
         regroup_w("o", 0, scopy)
         regroup_w("y", 1, vcopy)
         quantise_w("o", 0)
-        passes(0, 0)
+        passes(0, 0, 2, 2)
         quantise_w("y", 1)
         regroup_w("o", 1, vcopy)
         quantise_w("o", 1)
-        transposes_in(1, 0)
-        transposes_in(1, 1)
         copy_in(1, 0, vcopy)
         copy_in(1, 1, vcopy)
         quantise(1)

@@ -222,7 +222,11 @@ def tile_gatel0rdcell_pb_t_kernel(tc, x_t, h_t, Wy, by, Wo, bo, out):
         for t in range(GROUPS + 1):
             if ok(t):
                 activate(t, 0)
-                multiply(t, 0, 2, nc.gpsimd)
+                if t == GROUPS - 1:
+                    multiply(t, 0, 1, nc.vector)
+                    multiply(t, 1, 1, nc.vector)
+                else:
+                    multiply(t, 0, 2, nc.gpsimd)
             if ok(t + 2) and t > 0:
                 transposes_in(t + 2, 0)
             if ok(t - 2) and not tail(t - 1):
@@ -257,6 +261,14 @@ def tile_gatel0rdcell_pb_t_kernel(tc, x_t, h_t, Wy, by, Wo, bo, out):
                     for jl in range(GROUP):
                         copy_out(t - 1, jl, scopy if jl % 2 else vcopy)
                         store(t - 1, jl, 1)
+                elif t == GROUPS - 1:
+                    copy_out(t - 1, 0, vcopy)
+                    copy_out(t - 1, 1, vcopy)
+                    store(t - 1, 0, 2)
+                    multiply(t, 3, 1, nc.vector)
+                    copy_out(t - 1, 2, scopy)
+                    copy_out(t - 1, 3, scopy)
+                    store(t - 1, 2, 2)
                 else:
                     for jl in range(GROUP if tail(t) else 2):
                         copy_out(t - 1, jl, vcopy)
@@ -264,5 +276,5 @@ def tile_gatel0rdcell_pb_t_kernel(tc, x_t, h_t, Wy, by, Wo, bo, out):
                         store(t - 1, 0, GROUP)
             if ok(t + 2):
                 quantise(t + 2)
-            if ok(t):
+            if ok(t) and t < GROUPS - 1:
                 multiply(t, 3, 1, nc.gpsimd if t == 0 else nc.vector)

from contextlib import ExitStack

import concourse.mybir as mybir
from concourse.masks import make_identity

FP8X4 = mybir.dt.float8_e4m3fn_x4
BF16 = mybir.dt.bfloat16
F32 = mybir.dt.float32
U32 = mybir.dt.uint32
U8 = mybir.dt.uint8
ACT = mybir.ActivationFunctionType
ALU = mybir.AluOpType

P = 128
ROWS = 8192
HALF_K = 256
N_OUT = 512
TILES = ROWS // P
GROUP = 4
GROUPS = TILES // GROUP
GROWS = GROUP * P
BLOCKS = N_OUT // P
LOAD_CHUNKS = (1, 1, 1, 1, 2, 2, 4, 4)
FUNCS = (("y", ACT.Tanh), ("o", ACT.Sigmoid))

FLOPS = 2 * ROWS * (2 * HALF_K) * (2 * N_OUT)


def tile_gatel0rdcell_pb_t_kernel(tc, x_t, h_t, Wy, by, Wo, bo, out):
    nc = tc.nc
    x_v = x_t.rearrange("(p j) k -> p (j k)", j=TILES)
    h_v = h_t.rearrange("(p j) k -> p (j k)", j=TILES)
    out_v = out.rearrange("(p j) c -> p (j c)", j=TILES)

    with ExitStack() as ctx:
        const = ctx.enter_context(tc.tile_pool(name="const", bufs=1))
        stage = ctx.enter_context(tc.tile_pool(name="stage", bufs=3))
        work = ctx.enter_context(tc.tile_pool(name="work", bufs=4))
        psum_t = ctx.enter_context(tc.psum_pool(name="psum_t", bufs=4))
        psum_m = ctx.enter_context(tc.psum_pool(name="psum_m", bufs=4))
        ctx.enter_context(tc.manual_schedule())

        brow = const.tile([2 * BLOCKS, P], BF16, name="brow")
        brow32 = const.tile([P, P], F32, name="brow32")
        bias = const.tile([P, 2 * BLOCKS], F32, name="bias")
        warm = const.tile([P, 8], F32, name="warm")
        ident = const.tile([P, P], F32, name="ident")
        nc.scalar.dma_start(out=brow[0:BLOCKS, :], in_=by.rearrange("(r m) -> r m", r=BLOCKS))
        nc.scalar.dma_start(out=brow[BLOCKS : 2 * BLOCKS, :], in_=bo.rearrange("(r m) -> r m", r=BLOCKS))
        nc.vector.memset(warm[:], 0.0)
        nc.vector.memset(brow32[:], 0.0)
        make_identity(nc, ident[:])
        nc.scalar.activation(out=warm[:, 4:8], in_=warm[:, 0:4], func=ACT.Sigmoid)

        x_of = {}
        w_raw = {}

        def load_rows(first_group, n_groups):
            width = n_groups * GROUP * HALF_K
            lo = first_group * GROUP * HALF_K
            xs = const.tile([P, width], BF16, name="x%d" % first_group)
            hs = const.tile([P, width], BF16, name="h%d" % first_group)
            nc.sync.dma_start(out=xs[:], in_=x_v[:, lo : lo + width])
            nc.sync.dma_start(out=hs[:], in_=h_v[:, lo : lo + width])
            for i in range(n_groups):
                x_of[first_group + i] = (xs, hs, i)

        def load_w(key, w):
            raw = const.tile([P, 4 * N_OUT], BF16, name="raw_" + key)
            nc.sync.dma_start(
                out=raw[:].rearrange("p (u f) -> p u f", u=2),
                in_=w.rearrange("(u p e) n -> p u (e n)", u=2, e=2),
            )
            w_raw[key] = raw

        load_rows(0, LOAD_CHUNKS[0])
        load_w("y", Wy)
        load_w("o", Wo)
        first = LOAD_CHUNKS[0]
        for n_groups in LOAD_CHUNKS[1:]:
            load_rows(first, n_groups)
            first += n_groups

        banks = {}
        grouped = {}
        codes = {}
        acc = {}
        gate = {}
        turned = {}
        result = {}
        w_q = {}

        def ok(g):
            return 0 <= g < GROUPS

        def transposes_in(g, b):
            xs, hs, i = x_of[g]
            pt = psum_t.tile([P, 2, 2 * P], F32, name="pt", tag="pt")
            for u, src in enumerate((xs, hs)):
                words = src[:].bitcast(F32)
                for jl in range(2):
                    j = i * GROUP + 2 * b + jl
                    nc.tensor.transpose(pt[:, u, jl * P : (jl + 1) * P], words[:, j * P : (j + 1) * P], ident[:])
            banks[(g, b)] = pt

        def copy_in(g, b, engine_copy):
            if g not in grouped:
                gr = stage.tile([P, 4 * GROWS], BF16, name="gr", tag="gr", align_bytes=64)
                grouped[g] = gr
            words = grouped[g][:].bitcast(F32).rearrange("p (n u) -> p n u", u=2)
            engine_copy(out=words[:, 2 * P * b : 2 * P * (b + 1), :], in_=banks[(g, b)][:].rearrange("p u n -> p n u"))

        def quantise(g):
            cw = stage.tile([P, GROWS], U32, name="cw", tag="cw", align_bytes=64)
            cs = stage.tile([P, GROWS], U8, name="cs", tag="cs", align_bytes=64)
            nc.vector.quantize_mx(out=cw[:].bitcast(FP8X4), scales=cs[:], in_=grouped[g][:])
            codes[g] = (cw, cs)

        def regroup_w(key, h, engine_copy):
            gw = const.tile([P, 2 * N_OUT], BF16, name="gw_%s%d" % (key, h), align_bytes=64)
            half = w_raw[key][:].rearrange("p (t n) -> p t n", t=4)[:, :, h * 2 * P : (h + 1) * 2 * P]
            engine_copy(
                out=gw[:].rearrange("p (c i t) -> p c t i", i=4, t=4),
                in_=half.rearrange("p t (c i) -> p c t i", i=4),
            )
            grouped[(key, h)] = gw

        def quantise_w(key, h):
            cw = const.tile([P, 2 * P], U32, name="wcw_%s%d" % (key, h), align_bytes=64)
            cs = const.tile([P, 2 * P], U8, name="wcs_%s%d" % (key, h), align_bytes=64)
            nc.vector.quantize_mx(out=cw[:].bitcast(FP8X4), scales=cs[:], in_=grouped[(key, h)][:])
            w_q[(key, h)] = (cw, cs)

        def order_of(g, h):
            blocks = (2 * h, 2 * h + 1)
            if g == 0:
                return [(c, f) for f in range(2) for c in blocks]
            return [(c, f) for c in blocks for f in range(2)]

        def passes(g, h, first=0, n=4):
            cw, cs = codes[g]
            for c, f in order_of(g, h)[first : first + n]:
                wc, ws = w_q[(FUNCS[f][0], h)]
                lo = (c - 2 * h) * P
                a = psum_m.tile([P, GROWS], F32, name="acc", tag="acc")
                nc.tensor.matmul_mx(
                    out=a[:],
                    lhsT=wc[:, lo : lo + P].bitcast(FP8X4),
                    lhsT_scale=ws[:, lo : lo + P],
                    rhs=cw[:].bitcast(FP8X4),
                    rhs_scale=cs[:],
                    start=True,
                    stop=True,
                )
                acc[(g, c, f)] = a

        def activate(g, h):
            if g not in gate:
                ty = work.tile([P, BLOCKS * GROWS], F32, name="ty", tag="ty")
                to = work.tile([P, BLOCKS * GROWS], F32, name="to", tag="to")
                gate[g] = (ty, to)
            for c, f in order_of(g, h):
                nc.scalar.activation(
                    out=gate[g][f][:, c * GROWS : (c + 1) * GROWS],
                    in_=acc[(g, c, f)][:],
                    func=FUNCS[f][1],
                    bias=bias[:, f * BLOCKS + c : f * BLOCKS + c + 1],
                )

        def multiply(g, c, n, engine):
            sl = slice(c * GROWS, (c + n) * GROWS)
            engine.tensor_tensor(out=gate[g][0][:, sl], in0=gate[g][0][:, sl], in1=gate[g][1][:, sl], op=ALU.mult)

        def transposes_out(g, jl):
            po = psum_t.tile([P, N_OUT], F32, name="po", tag="pt")
            for c in range(BLOCKS):
                lo = c * GROWS + jl * P
                nc.tensor.transpose(po[:, c * P : (c + 1) * P], gate[g][0][:, lo : lo + P], ident[:])
            turned[(g, jl)] = po

        def copy_out(g, jl, engine_copy):
            if g not in result:
                res = work.tile([P, GROUP * N_OUT], F32, name="res", tag="res")
                result[g] = res
            engine_copy(out=result[g][:, jl * N_OUT : (jl + 1) * N_OUT], in_=turned[(g, jl)][:])

        def store(g, jl, n):
            d0 = (g * GROUP + jl) * N_OUT
            nc.sync.dma_start(out=out_v[:, d0 : d0 + n * N_OUT], in_=result[g][:, jl * N_OUT : (jl + n) * N_OUT])

        vcopy = nc.vector.tensor_copy
        scopy = nc.scalar.copy

        nc.vector.tensor_copy(out=brow32[0 : 2 * BLOCKS, :], in_=brow[:])
        pb = psum_m.tile([P, GROWS], F32, name="acc", tag="acc")
        nc.tensor.transpose(pb[:, 0:P], brow32[:], ident[:])
        nc.vector.tensor_copy(out=bias[:], in_=pb[:, 0 : 2 * BLOCKS])
        transposes_in(0, 0)
        transposes_in(0, 1)
        copy_in(0, 0, scopy)
        copy_in(0, 1, scopy)
        regroup_w("y", 0, vcopy)
        quantise_w("y", 0)
        quantise(0)
        passes(0, 0, 0, 2)
        transposes_in(1, 0)
        transposes_in(1, 1)
        regroup_w("o", 0, scopy)
        regroup_w("y", 1, vcopy)
        quantise_w("o", 0)
        passes(0, 0, 2, 2)
        quantise_w("y", 1)
        regroup_w("o", 1, vcopy)
        quantise_w("o", 1)
        copy_in(1, 0, vcopy)
        copy_in(1, 1, vcopy)
        quantise(1)

        def tail(t):
            return t + 2 >= GROUPS

        for t in range(GROUPS + 1):
            if ok(t):
                activate(t, 0)
                if t == GROUPS - 1:
                    multiply(t, 0, 1, nc.vector)
                    multiply(t, 1, 1, nc.vector)
                else:
                    multiply(t, 0, 2, nc.gpsimd)
            if ok(t + 2) and t > 0:
                transposes_in(t + 2, 0)
            if ok(t - 2) and not tail(t - 1):
                transposes_out(t - 2, 2)
                transposes_out(t - 2, 3)
            if ok(t):
                passes(t, 1)
            if ok(t + 2) and t > 0:
                copy_in(t + 2, 0, vcopy)
            if ok(t - 2) and not tail(t - 1):
                copy_out(t - 2, 2, vcopy)
                copy_out(t - 2, 3, vcopy)
                store(t - 2, 0, GROUP)
            if ok(t):
                activate(t, 1)
                multiply(t, 2, 1, nc.gpsimd)
            if ok(t + 2):
                if t == 0:
                    transposes_in(t + 2, 0)
                transposes_in(t + 2, 1)
            if ok(t - 1):
                for jl in range(GROUP if tail(t) else 2):
                    transposes_out(t - 1, jl)
            if ok(t + 1):
                passes(t + 1, 0)
            if ok(t + 2):
                if t == 0:
                    copy_in(t + 2, 0, vcopy)
                copy_in(t + 2, 1, vcopy)
            if ok(t - 1):
                if t == GROUPS:
                    for jl in range(GROUP):
                        copy_out(t - 1, jl, scopy if jl % 2 else vcopy)
                        store(t - 1, jl, 1)
                elif t == GROUPS - 1:
                    copy_out(t - 1, 0, vcopy)
                    copy_out(t - 1, 1, vcopy)
                    store(t - 1, 0, 2)
                    multiply(t, 3, 1, nc.vector)
                    copy_out(t - 1, 2, scopy)
                    copy_out(t - 1, 3, scopy)
                    store(t - 1, 2, 2)
                else:
                    for jl in range(GROUP if tail(t) else 2):
                        copy_out(t - 1, jl, vcopy)
                    if tail(t):
                        store(t - 1, 0, GROUP)
            if ok(t + 2):
                quantise(t + 2)
            if ok(t) and t < GROUPS - 1:
                multiply(t, 3, 1, nc.gpsimd if t == 0 else nc.vector)
